import numpy as np
import ml_dtypes


def mxq(x, axis, fmt="e4m3"):
    dtype, down = {"e4m3": (ml_dtypes.float8_e4m3fn, 7), "e5m2": (ml_dtypes.float8_e5m2, 14)}[fmt]
    v = np.moveaxis(np.asarray(x, np.float32).astype(ml_dtypes.bfloat16).astype(np.float64), axis, -1)
    blocks = v.reshape(v.shape[:-1] + (-1, 32))
    amax = np.abs(blocks).max(-1, keepdims=True)
    byte = np.maximum(np.where(amax > 0, np.frexp(amax)[1] - 1 + 127, 0) - down, 1)
    scale = np.exp2(byte - 127.0)
    codes = (blocks / scale).astype(np.float32).astype(dtype).astype(np.float64)
    return np.moveaxis((codes * scale).reshape(v.shape), -1, axis)


WIDE = False


def mx_kscale(k):
    if not WIDE:
        return np.ones(k)
    levels = np.array([10, -10, 5, -5, 0])
    if k % 512:
        return np.exp2(np.random.permutation(np.resize(levels, k // 32))).repeat(32)
    a = np.empty((k // 512, 16))
    for p in range(k // 512):
        a[p, :8] = np.random.permutation(np.resize(levels, 8))
        for g in range(8):
            far = levels[np.abs(levels - a[p, g]) >= 10]
            a[p, g + 8] = far[np.random.randint(len(far))]
    return np.exp2(a.ravel()).repeat(32)


BF16 = ml_dtypes.bfloat16


def bf(x):
    return np.asarray(x, np.float32).astype(BF16)


def f64(x):
    return np.asarray(x).astype(np.float64)


B, A, G, H1, H2 = 8192, 128, 5, 1024, 512
SLOPE = 0.4


def leaky(v):
    return np.where(v >= 0.0, v, SLOPE * v)


def setup_inputs():
    s, t = mx_kscale(H1), mx_kscale(H2)
    keep = np.where(np.random.uniform(size=(B, A)) > 0.2, 1.0, 0.0)
    return {"x": bf(np.random.standard_normal((B, A * G)) * np.repeat(keep, G, axis=1)),
            "h1": bf(leaky(np.random.standard_normal((B, H1))) * s),
            "W2": bf(np.random.standard_normal((H1, H2)) * 1.3 / np.sqrt(H1) / s[:, None] * t),
            "b2": bf(np.random.standard_normal(H2) * 0.3 * t),
            "W3": bf(np.random.standard_normal((H2, A)) * 2.5 / np.sqrt(H2) / t[:, None]),
            "b3": bf(np.random.standard_normal(A) * 0.5)}


def reference(x, h1, W2, b2, W3, b3):
    gsum = f64(x).reshape(B, A, G).sum(axis=-1)
    mask = gsum != 0.0
    h2 = leaky((mxq(f64(h1), 1, "e4m3") @ mxq(f64(W2), 0, "e4m3")) + f64(b2))
    logits = (mxq(h2, 1, "e4m3") @ mxq(f64(W3), 0, "e4m3")) + f64(b3)
    logits = np.where(mask, logits, -np.inf)
    e = np.exp(logits - logits.max(axis=1, keepdims=True))
    return e / e.sum(axis=1, keepdims=True)

@@ -1,0 +1,273 @@
+from contextlib import ExitStack
+
+import concourse.mybir as mybir
+from concourse.masks import make_identity
+
+F32 = mybir.dt.float32
+BF16 = mybir.dt.bfloat16
+U32 = mybir.dt.uint32
+U8 = mybir.dt.uint8
+FP8X4 = mybir.dt.float8_e4m3fn_x4
+ALU = mybir.AluOpType
+ACT = mybir.ActivationFunctionType
+AX = mybir.AxisListType
+
+P = 128
+PACK = 4
+B, A, G, H1, H2 = 8192, 128, 5, 1024, 512
+SLOPE = 0.4
+FORBID = -1.0e30
+PASSES = H1 // (P * PACK)
+TILES = 4
+ROWS = P * TILES
+UNITS = B // ROWS
+AHEAD = 3
+FOUR_TERM_UNITS = 9
+FLOPS = 2 * B * (H1 * H2 + H2 * A)
+
+
+def tile_dqn_pa_t_kernel(tc, x, h1, W2, b2, W3, b3, out):
+    nc = tc.nc
+    with ExitStack() as ctx:
+        const = ctx.enter_context(tc.tile_pool(name="const", bufs=1))
+        loads = ctx.enter_context(tc.tile_pool(name="loads", bufs=AHEAD + 1))
+        work = ctx.enter_context(tc.tile_pool(name="work", bufs=3))
+        psum = ctx.enter_context(tc.psum_pool(name="psum", bufs=1))
+        ctx.enter_context(tc.manual_schedule())
+        held = {}
+
+        def load(u):
+            rows = slice(ROWS * u, ROWS * (u + 1))
+            h1_sb = loads.tile([P, TILES, H1], BF16, tag="h1")
+            nc.sync.dma_start(out=h1_sb[:], in_=h1[rows, :].rearrange("(j p) k -> p j k", p=P))
+            x_sb = loads.tile([P, TILES, A * G], BF16, tag="x")
+            nc.sync.dma_start(out=x_sb[:], in_=x[rows, :].rearrange("(p j) c -> p j c", j=TILES))
+            held["h1", u] = h1_sb
+            held["x", u] = x_sb[:].rearrange("p j (a e) -> p (j a) e", e=G)
+
+        w2_raw = const.tile([P, PASSES, PACK * H2], BF16)
+        nc.sync.dma_start(out=w2_raw[:], in_=W2.rearrange("(s q v) n -> q s (v n)", s=PASSES, v=PACK))
+        for u in range(AHEAD):
+            load(u)
+        w3_raw = const.tile([P, PACK, A], BF16)
+        nc.scalar.dma_start(out=w3_raw[:], in_=W3.rearrange("(p t) a -> p t a", t=PACK))
+        b2_bf = const.tile([P, PACK], BF16)
+        nc.scalar.dma_start(out=b2_bf[:], in_=b2.rearrange("(p t) -> p t", t=PACK))
+        b3_bf = const.tile([P, A], BF16)
+        nc.scalar.dma_start(out=b3_bf[:], in_=b3.partition_broadcast(P))
+
+        ident_f32 = const.tile([P, P], F32)
+        make_identity(nc, ident_f32[:])
+        ident_bf = const.tile([P, P], BF16)
+        make_identity(nc, ident_bf[:])
+
+        w2_grouped = const.tile([P, PASSES, PACK * H2], BF16, align_bytes=64)
+        w2_words = const.tile([P, PASSES, H2], U32, align_bytes=64)
+        w2_scales = const.tile([P, PASSES, H2], U8, align_bytes=64)
+        for s, copy in ((0, nc.vector.tensor_copy), (1, nc.scalar.copy)):
+            copy(
+                out=w2_grouped[:, s, :].rearrange("q (t m v) -> q t m v", t=PACK, v=PACK),
+                in_=w2_raw[:, s, :].rearrange("q (v m t) -> q t m v", v=PACK, t=PACK),
+            )
+        w3_grouped = const.tile([P, A, PACK], BF16, align_bytes=64)
+        w3_words = const.tile([P, A], U32, align_bytes=64)
+        w3_scales = const.tile([P, A], U8, align_bytes=64)
+        nc.vector.tensor_copy(out=w3_grouped[:], in_=w3_raw[:].rearrange("p t a -> p a t"))
+        b2_f32 = const.tile([P, PACK], F32)
+        nc.vector.tensor_copy(out=b2_f32[:], in_=b2_bf[:])
+        b3_f32 = const.tile([P, A], F32)
+        nc.vector.tensor_copy(out=b3_f32[:], in_=b3_bf[:])
+        for s in range(PASSES):
+            nc.vector.quantize_mx(
+                out=w2_words[:, s, :].bitcast(FP8X4), scales=w2_scales[:, s, :], in_=w2_grouped[:, s, :]
+            )
+        nc.vector.quantize_mx(
+            out=w3_words[:].bitcast(FP8X4), scales=w3_scales[:], in_=w3_grouped[:].rearrange("p a t -> p (a t)")
+        )
+
+        def transpose_h1(u):
+            banks = []
+            for s in range(PASSES):
+                for half in range(TILES // 2):
+                    bank = psum.tile([P, 2, 2, P], F32, tag="bank", bufs=6)
+                    for j in range(2):
+                        for w in range(2):
+                            nc.tensor.transpose(
+                                bank[:, j, w, :],
+                                held["h1", u][:, 2 * half + j, :].bitcast(F32)[:, 2 * P * s + w : 2 * P * (s + 1) : 2],
+                                ident_f32[:],
+                            )
+                    banks.append(bank)
+            held["h1T", u] = banks
+
+        def copy_h1T(u):
+            grouped = work.tile([P, PASSES, PACK * ROWS], BF16, align_bytes=64, tag="grouped", bufs=2)
+            for s in range(PASSES):
+                words = grouped[:, s, :].bitcast(F32).rearrange("p (j r w) -> p j r w", j=TILES, w=2)
+                for half in range(TILES // 2):
+                    nc.scalar.copy(
+                        out=words[:, 2 * half : 2 * half + 2],
+                        in_=held["h1T", u][(TILES // 2) * s + half][:].rearrange("p j w r -> p j r w"),
+                    )
+            held["grouped", u] = grouped
+
+        def quantise_h1(u):
+            h1_words = work.tile([P, PASSES, ROWS], U32, align_bytes=64, tag="h1_words")
+            h1_scales = work.tile([P, PASSES, ROWS], U8, align_bytes=64, tag="h1_scales")
+            for s in range(PASSES):
+                nc.vector.quantize_mx(
+                    out=h1_words[:, s, :].bitcast(FP8X4), scales=h1_scales[:, s, :], in_=held["grouped", u][:, s, :]
+                )
+            held["h1_words", u] = h1_words
+            held["h1_scales", u] = h1_scales
+
+        def first_product(u):
+            products = []
+            for t in range(PACK):
+                bank = psum.tile([P, ROWS], F32, tag="bank", bufs=6)
+                for s in range(PASSES):
+                    nc.tensor.matmul_mx(
+                        out=bank[:],
+                        lhsT=w2_words[:, s, P * t : P * (t + 1)].bitcast(FP8X4),
+                        lhsT_scale=w2_scales[:, s, P * t : P * (t + 1)],
+                        rhs=held["h1_words", u][:, s, :].bitcast(FP8X4),
+                        rhs_scale=held["h1_scales", u][:, s, :],
+                        start=(s == 0),
+                        stop=(s == PASSES - 1),
+                    )
+                products.append(bank)
+            held["products", u] = products
+
+        def add_b2(u):
+            v = work.tile([P, ROWS // 4, PACK, 4], F32, tag="v")
+            for t in range(PACK):
+                nc.scalar.activation(
+                    out=v[:, :, t, :],
+                    in_=held["products", u][t][:].rearrange("p (c i) -> p c i", i=4),
+                    func=ACT.Identity,
+                    bias=b2_f32[:, t : t + 1],
+                    scale=1.0,
+                )
+            held["v", u] = v
+
+        def leaky(u):
+            h2 = work.tile([P, TILES, PACK * P], BF16, align_bytes=64, tag="h2", bufs=2)
+            v = held["v", u][:].rearrange("p c t i -> p (c t) i")
+            nc.vector.scalar_tensor_tensor(
+                out=h2[:].rearrange("p i ct -> p ct i"), in0=v, scalar=SLOPE, in1=v, op0=ALU.mult, op1=ALU.max
+            )
+            held["h2", u] = h2
+
+        def quantise_h2(u):
+            h2_words = work.tile([P, ROWS], U32, align_bytes=64, tag="h2_words")
+            h2_scales = work.tile([P, ROWS], U8, align_bytes=64, tag="h2_scales")
+            nc.vector.quantize_mx(
+                out=h2_words[:].bitcast(FP8X4), scales=h2_scales[:], in_=held["h2", u][:].rearrange("p i ct -> p (i ct)")
+            )
+            held["h2_words", u] = h2_words
+            held["h2_scales", u] = h2_scales
+
+        def second_product(u):
+            logits = psum.tile([P, TILES, A], F32, tag="logits")
+            for j in range(TILES):
+                nc.tensor.matmul_mx(
+                    out=logits[:, j, :],
+                    lhsT=held["h2_words", u][:, P * j : P * (j + 1)].bitcast(FP8X4),
+                    lhsT_scale=held["h2_scales", u][:, P * j : P * (j + 1)],
+                    rhs=w3_words[:].bitcast(FP8X4),
+                    rhs_scale=w3_scales[:],
+                    start=True,
+                    stop=True,
+                )
+            held["logits", u] = logits
+
+        def sum_on_tensor(u):
+            terms = 4 if u < FOUR_TERM_UNITS else 3
+            part = psum.tile([P, ROWS], F32, tag="part")
+            for e in range(terms):
+                nc.tensor.matmul(
+                    out=part[:], lhsT=ident_bf[:], rhs=held["x", u][:, :, e], start=(e == 0), stop=(e == terms - 1)
+                )
+            held["four", u] = part
+
+        def sum_fourth(u):
+            if u >= FOUR_TERM_UNITS:
+                four = work.tile([P, ROWS], F32, tag="four")
+                nc.vector.tensor_tensor(out=four[:], in0=held["four", u][:], in1=held["x", u][:, :, 3], op=ALU.add)
+                held["four", u] = four
+
+        def compare(u):
+            zero = work.tile([P, TILES, A], F32, tag="zero", bufs=2)
+            nc.vector.scalar_tensor_tensor(
+                out=zero[:].rearrange("p j a -> p (j a)"), in0=held["x", u][:, :, 4], scalar=-1.0,
+                in1=held["four", u][:], op0=ALU.mult, op1=ALU.is_equal,
+            )
+            held["zero", u] = zero
+
+        def offsets(u):
+            offset = work.tile([P, TILES, A], F32, tag="offset", bufs=5)
+            nc.vector.scalar_tensor_tensor(
+                out=offset[:], in0=held["zero", u][:], scalar=FORBID,
+                in1=b3_f32[:].unsqueeze(1).to_broadcast([P, TILES, A]), op0=ALU.mult, op1=ALU.add,
+            )
+            held["offset", u] = offset
+
+        def masked_logits(u):
+            masked = work.tile([P, TILES, A], F32, tag="masked")
+            nc.vector.tensor_tensor(out=masked[:], in0=held["logits", u][:], in1=held["offset", u][:], op=ALU.add)
+            held["masked", u] = masked
+
+        def row_max(u):
+            minus_max = work.tile([P, TILES], F32, tag="minus_max")
+            nc.vector.tensor_reduce(out=minus_max[:], in_=held["masked", u][:], axis=AX.X, op=ALU.max, negate=True)
+            held["minus_max", u] = minus_max
+
+        def exponentials(u):
+            expo = work.tile([P, TILES, A], F32, tag="expo")
+            total = work.tile([P, TILES], F32, tag="total")
+            for j in range(TILES):
+                nc.scalar.activation(
+                    out=expo[:, j, :], in_=held["masked", u][:, j, :], func=ACT.Exp,
+                    bias=held["minus_max", u][:, j : j + 1], scale=1.0, accum_out=total[:, j : j + 1],
+                )
+            held["expo", u] = expo
+            held["total", u] = total
+
+        def reciprocals(u):
+            inverse = work.tile([P, TILES], F32, tag="inverse")
+            nc.vector.reciprocal(out=inverse[:], in_=held["total", u][:])
+            held["inverse", u] = inverse
+
+        def scale_and_store(u):
+            probs = work.tile([P, TILES, A], F32, tag="probs")
+            for j in range(TILES):
+                nc.scalar.activation(
+                    out=probs[:, j, :], in_=held["expo", u][:, j, :], func=ACT.Copy,
+                    scale=held["inverse", u][:, j : j + 1],
+                )
+            rows = slice(ROWS * u, ROWS * (u + 1))
+            nc.scalar.dma_start(out=out[rows, :].rearrange("(p j) a -> p j a", j=TILES), in_=probs[:])
+
+        def run(stage, u):
+            if 0 <= u < UNITS:
+                stage(u)
+
+        for k in range(-1, UNITS + 4):
+            run(load, k + AHEAD if k >= 0 else UNITS)
+            run(transpose_h1, k)
+            run(copy_h1T, k)
+            run(leaky, k - 2)
+            run(masked_logits, k - 3)
+            run(first_product, k - 1)
+            run(quantise_h2, k - 2)
+            run(add_b2, k - 1)
+            run(compare, k)
+            run(sum_on_tensor, k + 1)
+            run(row_max, k - 3)
+            run(second_product, k - 2)
+            run(quantise_h1, k)
+            run(offsets, k)
+            run(exponentials, k - 3)
+            run(reciprocals, k - 4)
+            run(scale_and_store, k - 4)
+            run(sum_fourth, k + 1)

@@ -85,31 +85,30 @@ def tile_dqn_pa_t_kernel(tc, x, h1, W2, b2, W3, b3, out):
             out=w3_words[:].bitcast(FP8X4), scales=w3_scales[:], in_=w3_grouped[:].rearrange("p a t -> p (a t)")
         )
 
-        def transpose_h1(u):
+        def transpose_h1(u, s):
             banks = []
-            for s in range(PASSES):
-                for half in range(TILES // 2):
-                    bank = psum.tile([P, 2, 2, P], F32, tag="bank", bufs=6)
-                    for j in range(2):
-                        for w in range(2):
-                            nc.tensor.transpose(
-                                bank[:, j, w, :],
-                                held["h1", u][:, 2 * half + j, :].bitcast(F32)[:, 2 * P * s + w : 2 * P * (s + 1) : 2],
-                                ident_f32[:],
-                            )
-                    banks.append(bank)
-            held["h1T", u] = banks
+            for half in range(TILES // 2):
+                bank = psum.tile([P, 2, 2, P], F32, tag="bank", bufs=6)
+                for j in range(2):
+                    for w in range(2):
+                        nc.tensor.transpose(
+                            bank[:, j, w, :],
+                            held["h1", u][:, 2 * half + j, :].bitcast(F32)[:, 2 * P * s + w : 2 * P * (s + 1) : 2],
+                            ident_f32[:],
+                        )
+                banks.append(bank)
+            held["h1T", u, s] = banks
 
-        def copy_h1T(u):
-            grouped = work.tile([P, PASSES, PACK * ROWS], BF16, align_bytes=64, tag="grouped", bufs=2)
-            for s in range(PASSES):
-                words = grouped[:, s, :].bitcast(F32).rearrange("p (j r w) -> p j r w", j=TILES, w=2)
-                for half in range(TILES // 2):
-                    nc.scalar.copy(
-                        out=words[:, 2 * half : 2 * half + 2],
-                        in_=held["h1T", u][(TILES // 2) * s + half][:].rearrange("p j w r -> p j r w"),
-                    )
-            held["grouped", u] = grouped
+        def copy_h1T(u, s):
+            if s == 0:
+                grouped = work.tile([P, PASSES, PACK * ROWS], BF16, align_bytes=64, tag="grouped", bufs=2)
+                held["grouped", u] = grouped
+            words = held["grouped", u][:, s, :].bitcast(F32).rearrange("p (j r w) -> p j r w", j=TILES, w=2)
+            for half in range(TILES // 2):
+                nc.scalar.copy(
+                    out=words[:, 2 * half : 2 * half + 2],
+                    in_=held["h1T", u, s][half][:].rearrange("p j w r -> p j r w"),
+                )
 
         def quantise_h1(u):
             h1_words = work.tile([P, PASSES, ROWS], U32, align_bytes=64, tag="h1_words")
@@ -121,9 +120,9 @@ def tile_dqn_pa_t_kernel(tc, x, h1, W2, b2, W3, b3, out):
             held["h1_words", u] = h1_words
             held["h1_scales", u] = h1_scales
 
-        def first_product(u):
-            products = []
-            for t in range(PACK):
+        def first_product(u, first_t):
+            products = held.setdefault(("products", u), [])
+            for t in range(first_t, first_t + 2):
                 bank = psum.tile([P, ROWS], F32, tag="bank", bufs=6)
                 for s in range(PASSES):
                     nc.tensor.matmul_mx(
@@ -136,11 +135,13 @@ def tile_dqn_pa_t_kernel(tc, x, h1, W2, b2, W3, b3, out):
                         stop=(s == PASSES - 1),
                     )
                 products.append(bank)
-            held["products", u] = products
 
-        def add_b2(u):
-            v = work.tile([P, ROWS // 4, PACK, 4], F32, tag="v")
-            for t in range(PACK):
+        def add_b2(u, first_t):
+            if first_t == 0:
+                v_new = work.tile([P, ROWS // 4, PACK, 4], F32, tag="v")
+                held["v", u] = v_new
+            v = held["v", u]
+            for t in range(first_t, first_t + 2):
                 nc.scalar.activation(
                     out=v[:, :, t, :],
                     in_=held["products", u][t][:].rearrange("p (c i) -> p c i", i=4),
@@ -148,7 +149,6 @@ def tile_dqn_pa_t_kernel(tc, x, h1, W2, b2, W3, b3, out):
                     bias=b2_f32[:, t : t + 1],
                     scale=1.0,
                 )
-            held["v", u] = v
 
         def leaky(u):
             h2 = work.tile([P, TILES, PACK * P], BF16, align_bytes=64, tag="h2", bufs=2)
@@ -248,19 +248,23 @@ def tile_dqn_pa_t_kernel(tc, x, h1, W2, b2, W3, b3, out):
             rows = slice(ROWS * u, ROWS * (u + 1))
             nc.scalar.dma_start(out=out[rows, :].rearrange("(p j) a -> p j a", j=TILES), in_=probs[:])
 
-        def run(stage, u):
+        def run(stage, u, *part):
             if 0 <= u < UNITS:
-                stage(u)
+                stage(u, *part)
 
         for k in range(-1, UNITS + 4):
             run(load, k + AHEAD if k >= 0 else UNITS)
-            run(transpose_h1, k)
-            run(copy_h1T, k)
+            run(transpose_h1, k, 0)
+            run(copy_h1T, k, 0)
             run(leaky, k - 2)
             run(masked_logits, k - 3)
-            run(first_product, k - 1)
+            run(first_product, k - 1, 0)
+            run(add_b2, k - 1, 0)
+            run(transpose_h1, k, 1)
+            run(copy_h1T, k, 1)
+            run(first_product, k - 1, 2)
             run(quantise_h2, k - 2)
-            run(add_b2, k - 1)
+            run(add_b2, k - 1, 2)
             run(compare, k)
             run(sum_on_tensor, k + 1)
             run(row_max, k - 3)

@@ -190,16 +190,16 @@ def tile_dqn_pa_t_kernel(tc, x, h1, W2, b2, W3, b3, out):
                 )
             held["four", u] = part
 
-        def sum_fourth(u):
+        def sum_last_two(u):
             if u >= FOUR_TERM_UNITS:
-                four = work.tile([P, ROWS], F32, tag="four")
-                nc.vector.tensor_tensor(out=four[:], in0=held["four", u][:], in1=held["x", u][:, :, 3], op=ALU.add)
-                held["four", u] = four
+                last_two = work.tile([P, ROWS], F32, tag="last_two", bufs=2)
+                nc.gpsimd.tensor_tensor(out=last_two[:], in0=held["x", u][:, :, 3], in1=held["x", u][:, :, 4], op=ALU.add)
+                held["last", u] = last_two[:]
 
         def compare(u):
             zero = work.tile([P, TILES, A], F32, tag="zero", bufs=2)
             nc.vector.scalar_tensor_tensor(
-                out=zero[:].rearrange("p j a -> p (j a)"), in0=held["x", u][:, :, 4], scalar=-1.0,
+                out=zero[:].rearrange("p j a -> p (j a)"), in0=held.get(("last", u), held["x", u][:, :, 4]), scalar=-1.0,
                 in1=held["four", u][:], op0=ALU.mult, op1=ALU.is_equal,
             )
             held["zero", u] = zero
@@ -274,4 +274,4 @@ def tile_dqn_pa_t_kernel(tc, x, h1, W2, b2, W3, b3, out):
             run(exponentials, k - 3)
             run(reciprocals, k - 4)
             run(scale_and_store, k - 4)
-            run(sum_fourth, k + 1)
+            run(sum_last_two, k + 1)

@@ -22,7 +22,7 @@ TILES = 4
 ROWS = P * TILES
 UNITS = B // ROWS
 AHEAD = 3
-FOUR_TERM_UNITS = 9
+THREE_TERM_UNITS = 7
 FLOPS = 2 * B * (H1 * H2 + H2 * A)
 
 
@@ -40,7 +40,7 @@ def tile_dqn_pa_t_kernel(tc, x, h1, W2, b2, W3, b3, out):
             rows = slice(ROWS * u, ROWS * (u + 1))
             h1_sb = loads.tile([P, TILES, H1], BF16, tag="h1")
             nc.sync.dma_start(out=h1_sb[:], in_=h1[rows, :].rearrange("(j p) k -> p j k", p=P))
-            x_sb = loads.tile([P, TILES, A * G], BF16, tag="x")
+            x_sb = loads.tile([P, TILES, A * G], BF16, tag="x", bufs=AHEAD + 2)
             nc.sync.dma_start(out=x_sb[:], in_=x[rows, :].rearrange("(p j) c -> p j c", j=TILES))
             held["h1", u] = h1_sb
             held["x", u] = x_sb[:].rearrange("p j (a e) -> p (j a) e", e=G)
@@ -182,7 +182,7 @@ def tile_dqn_pa_t_kernel(tc, x, h1, W2, b2, W3, b3, out):
             held["logits", u] = logits
 
         def sum_on_tensor(u):
-            terms = 4 if u < FOUR_TERM_UNITS else 3
+            terms = 3 if u < THREE_TERM_UNITS else 4
             part = psum.tile([P, ROWS], F32, tag="part")
             for e in range(terms):
                 nc.tensor.matmul(
@@ -191,7 +191,7 @@ def tile_dqn_pa_t_kernel(tc, x, h1, W2, b2, W3, b3, out):
             held["four", u] = part
 
         def sum_last_two(u):
-            if u >= FOUR_TERM_UNITS:
+            if u < THREE_TERM_UNITS:
                 last_two = work.tile([P, ROWS], F32, tag="last_two", bufs=2)
                 nc.gpsimd.tensor_tensor(out=last_two[:], in0=held["x", u][:, :, 3], in1=held["x", u][:, :, 4], op=ALU.add)
                 held["last", u] = last_two[:]
@@ -246,14 +246,14 @@ def tile_dqn_pa_t_kernel(tc, x, h1, W2, b2, W3, b3, out):
                     scale=held["inverse", u][:, j : j + 1],
                 )
             rows = slice(ROWS * u, ROWS * (u + 1))
-            nc.scalar.dma_start(out=out[rows, :].rearrange("(p j) a -> p j a", j=TILES), in_=probs[:])
+            nc.sync.dma_start(out=out[rows, :].rearrange("(p j) a -> p j a", j=TILES), in_=probs[:])
 
         def run(stage, u, *part):
             if 0 <= u < UNITS:
                 stage(u, *part)
 
-        for k in range(-1, UNITS + 4):
-            run(load, k + AHEAD if k >= 0 else UNITS)
+        for k in range(UNITS + 4):
+            run(load, k + AHEAD)
             run(transpose_h1, k, 0)
             run(copy_h1T, k, 0)
             run(leaky, k - 2)
@@ -265,13 +265,13 @@ def tile_dqn_pa_t_kernel(tc, x, h1, W2, b2, W3, b3, out):
             run(first_product, k - 1, 2)
             run(quantise_h2, k - 2)
             run(add_b2, k - 1, 2)
-            run(compare, k)
-            run(sum_on_tensor, k + 1)
+            run(compare, k - 1)
+            run(sum_on_tensor, k)
             run(row_max, k - 3)
             run(second_product, k - 2)
             run(quantise_h1, k)
-            run(offsets, k)
+            run(offsets, k - 1)
             run(exponentials, k - 3)
             run(reciprocals, k - 4)
             run(scale_and_store, k - 4)
-            run(sum_last_two, k + 1)
+            run(sum_last_two, k)

@@ -181,14 +181,16 @@ def tile_dqn_pa_t_kernel(tc, x, h1, W2, b2, W3, b3, out):
                 )
             held["logits", u] = logits
 
-        def sum_on_tensor(u):
+        def sum_on_tensor(u, first_e):
             terms = 3 if u < THREE_TERM_UNITS else 4
-            part = psum.tile([P, ROWS], F32, tag="part")
-            for e in range(terms):
+            if first_e == 0:
+                part = psum.tile([P, ROWS], F32, tag="part")
+                held["four", u] = part
+            for e in range(first_e, 2 if first_e == 0 else terms):
                 nc.tensor.matmul(
-                    out=part[:], lhsT=ident_bf[:], rhs=held["x", u][:, :, e], start=(e == 0), stop=(e == terms - 1)
+                    out=held["four", u][:], lhsT=ident_bf[:], rhs=held["x", u][:, :, e], start=(e == 0),
+                    stop=(e == terms - 1),
                 )
-            held["four", u] = part
 
         def sum_last_two(u):
             if u < THREE_TERM_UNITS:
@@ -254,24 +256,25 @@ def tile_dqn_pa_t_kernel(tc, x, h1, W2, b2, W3, b3, out):
 
         for k in range(UNITS + 4):
             run(load, k + AHEAD)
+            run(sum_last_two, k)
             run(transpose_h1, k, 0)
             run(copy_h1T, k, 0)
             run(leaky, k - 2)
+            run(sum_on_tensor, k, 0)
+            run(transpose_h1, k, 1)
+            run(copy_h1T, k, 1)
+            run(sum_on_tensor, k, 2)
             run(masked_logits, k - 3)
             run(first_product, k - 1, 0)
             run(add_b2, k - 1, 0)
-            run(transpose_h1, k, 1)
-            run(copy_h1T, k, 1)
             run(first_product, k - 1, 2)
             run(quantise_h2, k - 2)
             run(add_b2, k - 1, 2)
-            run(compare, k - 1)
-            run(sum_on_tensor, k)
             run(row_max, k - 3)
             run(second_product, k - 2)
             run(quantise_h1, k)
             run(offsets, k - 1)
+            run(compare, k)
             run(exponentials, k - 3)
             run(reciprocals, k - 4)
             run(scale_and_store, k - 4)
-            run(sum_last_two, k)

@@ -270,11 +270,11 @@ def tile_dqn_pa_t_kernel(tc, x, h1, W2, b2, W3, b3, out):
             run(first_product, k - 1, 2)
             run(quantise_h2, k - 2)
             run(add_b2, k - 1, 2)
+            run(compare, k)
             run(row_max, k - 3)
             run(second_product, k - 2)
             run(quantise_h1, k)
-            run(offsets, k - 1)
-            run(compare, k)
+            run(offsets, k)
             run(exponentials, k - 3)
             run(reciprocals, k - 4)
             run(scale_and_store, k - 4)

@@ -254,15 +254,17 @@ def tile_dqn_pa_t_kernel(tc, x, h1, W2, b2, W3, b3, out):
             if 0 <= u < UNITS:
                 stage(u, *part)
 
-        for k in range(UNITS + 4):
+        for k in range(UNITS + 5):
             run(load, k + AHEAD)
             run(sum_last_two, k)
             run(transpose_h1, k, 0)
             run(copy_h1T, k, 0)
+            run(exponentials, k - 4)
             run(leaky, k - 2)
             run(sum_on_tensor, k, 0)
             run(transpose_h1, k, 1)
             run(copy_h1T, k, 1)
+            run(scale_and_store, k - 5)
             run(sum_on_tensor, k, 2)
             run(masked_logits, k - 3)
             run(first_product, k - 1, 0)
@@ -275,6 +277,4 @@ def tile_dqn_pa_t_kernel(tc, x, h1, W2, b2, W3, b3, out):
             run(second_product, k - 2)
             run(quantise_h1, k)
             run(offsets, k)
-            run(exponentials, k - 3)
             run(reciprocals, k - 4)
-            run(scale_and_store, k - 4)

@@ -36,25 +36,30 @@ def tile_dqn_pa_t_kernel(tc, x, h1, W2, b2, W3, b3, out):
         ctx.enter_context(tc.manual_schedule())
         held = {}
 
-        def load(u):
+        def load_h1(u):
             rows = slice(ROWS * u, ROWS * (u + 1))
             h1_sb = loads.tile([P, TILES, H1], BF16, tag="h1")
             nc.sync.dma_start(out=h1_sb[:], in_=h1[rows, :].rearrange("(j p) k -> p j k", p=P))
+            held["h1", u] = h1_sb
+
+        def load_x(u):
+            rows = slice(ROWS * u, ROWS * (u + 1))
             x_sb = loads.tile([P, TILES, A * G], BF16, tag="x", bufs=AHEAD + 2)
             nc.sync.dma_start(out=x_sb[:], in_=x[rows, :].rearrange("(p j) c -> p j c", j=TILES))
-            held["h1", u] = h1_sb
             held["x", u] = x_sb[:].rearrange("p j (a e) -> p (j a) e", e=G)
 
+        load_h1(0)
         w2_raw = const.tile([P, PASSES, PACK * H2], BF16)
         nc.sync.dma_start(out=w2_raw[:], in_=W2.rearrange("(s q v) n -> q s (v n)", s=PASSES, v=PACK))
-        for u in range(AHEAD):
-            load(u)
-        w3_raw = const.tile([P, PACK, A], BF16)
-        nc.scalar.dma_start(out=w3_raw[:], in_=W3.rearrange("(p t) a -> p t a", t=PACK))
         b2_bf = const.tile([P, PACK], BF16)
-        nc.scalar.dma_start(out=b2_bf[:], in_=b2.rearrange("(p t) -> p t", t=PACK))
+        nc.sync.dma_start(out=b2_bf[:], in_=b2.rearrange("(p t) -> p t", t=PACK))
+        load_h1(1)
+        w3_raw = const.tile([P, PACK, A], BF16)
+        nc.sync.dma_start(out=w3_raw[:], in_=W3.rearrange("(p t) a -> p t a", t=PACK))
+        load_h1(2)
+        load_x(0)
         b3_bf = const.tile([P, A], BF16)
-        nc.scalar.dma_start(out=b3_bf[:], in_=b3.partition_broadcast(P))
+        nc.sync.dma_start(out=b3_bf[:], in_=b3.partition_broadcast(P))
 
         ident_f32 = const.tile([P, P], F32)
         make_identity(nc, ident_f32[:])
@@ -64,26 +69,30 @@ def tile_dqn_pa_t_kernel(tc, x, h1, W2, b2, W3, b3, out):
         w2_grouped = const.tile([P, PASSES, PACK * H2], BF16, align_bytes=64)
         w2_words = const.tile([P, PASSES, H2], U32, align_bytes=64)
         w2_scales = const.tile([P, PASSES, H2], U8, align_bytes=64)
-        for s, copy in ((0, nc.vector.tensor_copy), (1, nc.scalar.copy)):
+
+        def group_w2(s, copy):
             copy(
                 out=w2_grouped[:, s, :].rearrange("q (t m v) -> q t m v", t=PACK, v=PACK),
                 in_=w2_raw[:, s, :].rearrange("q (v m t) -> q t m v", v=PACK, t=PACK),
             )
-        w3_grouped = const.tile([P, A, PACK], BF16, align_bytes=64)
-        w3_words = const.tile([P, A], U32, align_bytes=64)
-        w3_scales = const.tile([P, A], U8, align_bytes=64)
-        nc.vector.tensor_copy(out=w3_grouped[:], in_=w3_raw[:].rearrange("p t a -> p a t"))
-        b2_f32 = const.tile([P, PACK], F32)
-        nc.vector.tensor_copy(out=b2_f32[:], in_=b2_bf[:])
-        b3_f32 = const.tile([P, A], F32)
-        nc.vector.tensor_copy(out=b3_f32[:], in_=b3_bf[:])
-        for s in range(PASSES):
+
+        def quantise_w2(s):
             nc.vector.quantize_mx(
                 out=w2_words[:, s, :].bitcast(FP8X4), scales=w2_scales[:, s, :], in_=w2_grouped[:, s, :]
             )
-        nc.vector.quantize_mx(
-            out=w3_words[:].bitcast(FP8X4), scales=w3_scales[:], in_=w3_grouped[:].rearrange("p a t -> p (a t)")
-        )
+
+        w3_grouped = const.tile([P, A, PACK], BF16, align_bytes=64)
+        w3_words = const.tile([P, A], U32, align_bytes=64)
+        w3_scales = const.tile([P, A], U8, align_bytes=64)
+        b2_f32 = const.tile([P, PACK], F32)
+        b3_f32 = const.tile([P, A], F32)
+
+        def prepare_w3_and_b3():
+            nc.vector.tensor_copy(out=w3_grouped[:], in_=w3_raw[:].rearrange("p t a -> p a t"))
+            nc.vector.tensor_copy(out=b3_f32[:], in_=b3_bf[:])
+            nc.vector.quantize_mx(
+                out=w3_words[:].bitcast(FP8X4), scales=w3_scales[:], in_=w3_grouped[:].rearrange("p a t -> p (a t)")
+            )
 
         def transpose_h1(u, s):
             banks = []
@@ -254,27 +263,36 @@ def tile_dqn_pa_t_kernel(tc, x, h1, W2, b2, W3, b3, out):
             if 0 <= u < UNITS:
                 stage(u, *part)
 
+        group_w2(0, nc.vector.tensor_copy)
+        nc.vector.tensor_copy(out=b2_f32[:], in_=b2_bf[:])
+        quantise_w2(0)
         for k in range(UNITS + 5):
-            run(load, k + AHEAD)
-            run(sum_last_two, k)
+            run(load_h1, k + AHEAD)
+            run(load_x, k + 1)
+            run(sum_last_two, k - 2)
             run(transpose_h1, k, 0)
             run(copy_h1T, k, 0)
             run(exponentials, k - 4)
             run(leaky, k - 2)
-            run(sum_on_tensor, k, 0)
+            run(sum_on_tensor, k - 2, 0)
             run(transpose_h1, k, 1)
             run(copy_h1T, k, 1)
             run(scale_and_store, k - 5)
-            run(sum_on_tensor, k, 2)
+            run(sum_on_tensor, k - 2, 2)
             run(masked_logits, k - 3)
             run(first_product, k - 1, 0)
             run(add_b2, k - 1, 0)
             run(first_product, k - 1, 2)
             run(quantise_h2, k - 2)
             run(add_b2, k - 1, 2)
-            run(compare, k)
+            run(compare, k - 2)
             run(row_max, k - 3)
             run(second_product, k - 2)
             run(quantise_h1, k)
-            run(offsets, k)
+            if k == 0:
+                group_w2(1, nc.scalar.copy)
+                quantise_w2(1)
+            if k == 1:
+                prepare_w3_and_b3()
+            run(offsets, k - 2)
             run(reciprocals, k - 4)

@@ -16,7 +16,7 @@ P = 128
 PACK = 4
 B, A, G, H1, H2 = 8192, 128, 5, 1024, 512
 SLOPE = 0.4
-FORBID = -1.0e30
+UNIT = 2.0**64
 PASSES = H1 // (P * PACK)
 TILES = 4
 ROWS = P * TILES
@@ -85,11 +85,14 @@ def tile_dqn_pa_t_kernel(tc, x, h1, W2, b2, W3, b3, out):
         w3_words = const.tile([P, A], U32, align_bytes=64)
         w3_scales = const.tile([P, A], U8, align_bytes=64)
         b2_f32 = const.tile([P, PACK], F32)
-        b3_f32 = const.tile([P, A], F32)
+        b3_units = const.tile([P, TILES, A], BF16)
 
         def prepare_w3_and_b3():
             nc.vector.tensor_copy(out=w3_grouped[:], in_=w3_raw[:].rearrange("p t a -> p a t"))
-            nc.vector.tensor_copy(out=b3_f32[:], in_=b3_bf[:])
+            nc.vector.tensor_scalar(
+                out=b3_units[:], in0=b3_bf[:].unsqueeze(1).to_broadcast([P, TILES, A]), scalar1=1.0 / UNIT, scalar2=None,
+                op0=ALU.mult,
+            )
             nc.vector.quantize_mx(
                 out=w3_words[:].bitcast(FP8X4), scales=w3_scales[:], in_=w3_grouped[:].rearrange("p a t -> p (a t)")
             )
@@ -208,7 +211,7 @@ def tile_dqn_pa_t_kernel(tc, x, h1, W2, b2, W3, b3, out):
                 held["last", u] = last_two[:]
 
         def compare(u):
-            zero = work.tile([P, TILES, A], F32, tag="zero", bufs=2)
+            zero = work.tile([P, TILES, A], BF16, tag="zero", bufs=2)
             nc.vector.scalar_tensor_tensor(
                 out=zero[:].rearrange("p j a -> p (j a)"), in0=held.get(("last", u), held["x", u][:, :, 4]), scalar=-1.0,
                 in1=held["four", u][:], op0=ALU.mult, op1=ALU.is_equal,
@@ -216,16 +219,15 @@ def tile_dqn_pa_t_kernel(tc, x, h1, W2, b2, W3, b3, out):
             held["zero", u] = zero
 
         def offsets(u):
-            offset = work.tile([P, TILES, A], F32, tag="offset", bufs=5)
-            nc.vector.scalar_tensor_tensor(
-                out=offset[:], in0=held["zero", u][:], scalar=FORBID,
-                in1=b3_f32[:].unsqueeze(1).to_broadcast([P, TILES, A]), op0=ALU.mult, op1=ALU.add,
-            )
+            offset = work.tile([P, TILES, A], BF16, tag="offset", bufs=5)
+            nc.vector.tensor_tensor(out=offset[:], in0=b3_units[:], in1=held["zero", u][:], op=ALU.subtract)
             held["offset", u] = offset
 
         def masked_logits(u):
             masked = work.tile([P, TILES, A], F32, tag="masked")
-            nc.vector.tensor_tensor(out=masked[:], in0=held["logits", u][:], in1=held["offset", u][:], op=ALU.add)
+            nc.vector.scalar_tensor_tensor(
+                out=masked[:], in0=held["logits", u][:], scalar=1.0 / UNIT, in1=held["offset", u][:], op0=ALU.mult, op1=ALU.add
+            )
             held["masked", u] = masked
 
         def row_max(u):
@@ -233,13 +235,18 @@ def tile_dqn_pa_t_kernel(tc, x, h1, W2, b2, W3, b3, out):
             nc.vector.tensor_reduce(out=minus_max[:], in_=held["masked", u][:], axis=AX.X, op=ALU.max, negate=True)
             held["minus_max", u] = minus_max
 
+        def scale_max(u):
+            bias = work.tile([P, TILES], F32, tag="bias")
+            nc.scalar.activation(out=bias[:], in_=held["minus_max", u][:], func=ACT.Copy, scale=UNIT)
+            held["bias", u] = bias
+
         def exponentials(u):
             expo = work.tile([P, TILES, A], F32, tag="expo")
             total = work.tile([P, TILES], F32, tag="total")
             for j in range(TILES):
                 nc.scalar.activation(
                     out=expo[:, j, :], in_=held["masked", u][:, j, :], func=ACT.Exp,
-                    bias=held["minus_max", u][:, j : j + 1], scale=1.0, accum_out=total[:, j : j + 1],
+                    bias=held["bias", u][:, j : j + 1], scale=UNIT, accum_out=total[:, j : j + 1],
                 )
             held["expo", u] = expo
             held["total", u] = total
@@ -271,6 +278,7 @@ def tile_dqn_pa_t_kernel(tc, x, h1, W2, b2, W3, b3, out):
             run(load_x, k + 1)
             run(sum_last_two, k - 2)
             run(transpose_h1, k, 0)
+            run(scale_max, k - 4)
             run(copy_h1T, k, 0)
             run(exponentials, k - 4)
             run(leaky, k - 2)

@@ -125,10 +125,11 @@ def tile_dqn_pa_t_kernel(tc, x, h1, W2, b2, W3, b3, out):
         def quantise_h1(u):
             h1_words = work.tile([P, PASSES, ROWS], U32, align_bytes=64, tag="h1_words")
             h1_scales = work.tile([P, PASSES, ROWS], U8, align_bytes=64, tag="h1_scales")
-            for s in range(PASSES):
-                nc.vector.quantize_mx(
-                    out=h1_words[:, s, :].bitcast(FP8X4), scales=h1_scales[:, s, :], in_=held["grouped", u][:, s, :]
-                )
+            nc.vector.quantize_mx(
+                out=h1_words[:].rearrange("p s r -> p (s r)").bitcast(FP8X4),
+                scales=h1_scales[:].rearrange("p s r -> p (s r)"),
+                in_=held["grouped", u][:].rearrange("p s rt -> p (s rt)"),
+            )
             held["h1_words", u] = h1_words
             held["h1_scales", u] = h1_scales
 

@@ -97,30 +97,26 @@ def tile_dqn_pa_t_kernel(tc, x, h1, W2, b2, W3, b3, out):
                 out=w3_words[:].bitcast(FP8X4), scales=w3_scales[:], in_=w3_grouped[:].rearrange("p a t -> p (a t)")
             )
 
-        def transpose_h1(u, s):
-            banks = []
-            for half in range(TILES // 2):
-                bank = psum.tile([P, 2, 2, P], F32, tag="bank", bufs=6)
-                for j in range(2):
-                    for w in range(2):
-                        nc.tensor.transpose(
-                            bank[:, j, w, :],
-                            held["h1", u][:, 2 * half + j, :].bitcast(F32)[:, 2 * P * s + w : 2 * P * (s + 1) : 2],
-                            ident_f32[:],
-                        )
-                banks.append(bank)
-            held["h1T", u, s] = banks
+        def transpose_h1(u, s, half):
+            bank = psum.tile([P, 2, 2, P], F32, tag="bank", bufs=6)
+            for j in range(2):
+                for w in range(2):
+                    nc.tensor.transpose(
+                        bank[:, j, w, :],
+                        held["h1", u][:, 2 * half + j, :].bitcast(F32)[:, 2 * P * s + w : 2 * P * (s + 1) : 2],
+                        ident_f32[:],
+                    )
+            held["h1T", u, s, half] = bank
 
-        def copy_h1T(u, s):
-            if s == 0:
+        def copy_h1T(u, s, half):
+            if s == 0 and half == 0:
                 grouped = work.tile([P, PASSES, PACK * ROWS], BF16, align_bytes=64, tag="grouped", bufs=2)
                 held["grouped", u] = grouped
             words = held["grouped", u][:, s, :].bitcast(F32).rearrange("p (j r w) -> p j r w", j=TILES, w=2)
-            for half in range(TILES // 2):
-                nc.scalar.copy(
-                    out=words[:, 2 * half : 2 * half + 2],
-                    in_=held["h1T", u, s][half][:].rearrange("p j w r -> p j r w"),
-                )
+            nc.scalar.copy(
+                out=words[:, 2 * half : 2 * half + 2],
+                in_=held["h1T", u, s, half][:].rearrange("p j w r -> p j r w"),
+            )
 
         def quantise_h1(u):
             h1_words = work.tile([P, PASSES, ROWS], U32, align_bytes=64, tag="h1_words")
@@ -194,12 +190,12 @@ def tile_dqn_pa_t_kernel(tc, x, h1, W2, b2, W3, b3, out):
                 )
             held["logits", u] = logits
 
-        def sum_on_tensor(u, first_e):
+        def sum_on_tensor(u, e):
             terms = 3 if u < THREE_TERM_UNITS else 4
-            if first_e == 0:
+            if e == 0:
                 part = psum.tile([P, ROWS], F32, tag="part")
                 held["four", u] = part
-            for e in range(first_e, 2 if first_e == 0 else terms):
+            if e < terms:
                 nc.tensor.matmul(
                     out=held["four", u][:], lhsT=ident_bf[:], rhs=held["x", u][:, :, e], start=(e == 0),
                     stop=(e == terms - 1),
@@ -278,16 +274,22 @@ def tile_dqn_pa_t_kernel(tc, x, h1, W2, b2, W3, b3, out):
             run(load_h1, k + AHEAD)
             run(load_x, k + 1)
             run(sum_last_two, k - 2)
-            run(transpose_h1, k, 0)
-            run(scale_max, k - 4)
-            run(copy_h1T, k, 0)
-            run(exponentials, k - 4)
             run(leaky, k - 2)
+            run(scale_max, k - 4)
+            run(transpose_h1, k, 0, 0)
+            run(copy_h1T, k, 0, 0)
             run(sum_on_tensor, k - 2, 0)
-            run(transpose_h1, k, 1)
-            run(copy_h1T, k, 1)
-            run(scale_and_store, k - 5)
+            run(transpose_h1, k, 0, 1)
+            run(copy_h1T, k, 0, 1)
+            run(exponentials, k - 4)
+            run(sum_on_tensor, k - 2, 1)
+            run(transpose_h1, k, 1, 0)
+            run(copy_h1T, k, 1, 0)
             run(sum_on_tensor, k - 2, 2)
+            run(transpose_h1, k, 1, 1)
+            run(copy_h1T, k, 1, 1)
+            run(scale_and_store, k - 5)
+            run(sum_on_tensor, k - 2, 3)
             run(masked_logits, k - 3)
             run(first_product, k - 1, 0)
             run(add_b2, k - 1, 0)

@@ -160,7 +160,7 @@ def tile_dqn_pa_t_kernel(tc, x, h1, W2, b2, W3, b3, out):
                 )
 
         def leaky(u):
-            h2 = work.tile([P, TILES, PACK * P], BF16, align_bytes=64, tag="h2", bufs=2)
+            h2 = work.tile([P, TILES, PACK * P], BF16, align_bytes=64, tag="h2", bufs=3)
             v = held["v", u][:].rearrange("p c t i -> p (c t) i")
             nc.vector.scalar_tensor_tensor(
                 out=h2[:].rearrange("p i ct -> p ct i"), in0=v, scalar=SLOPE, in1=v, op0=ALU.mult, op1=ALU.max
@@ -203,15 +203,21 @@ def tile_dqn_pa_t_kernel(tc, x, h1, W2, b2, W3, b3, out):
 
         def sum_last_two(u):
             if u < THREE_TERM_UNITS:
-                last_two = work.tile([P, ROWS], F32, tag="last_two", bufs=2)
+                last_two = work.tile([P, ROWS], F32, align_bytes=64, tag="h2", bufs=3)
                 nc.gpsimd.tensor_tensor(out=last_two[:], in0=held["x", u][:, :, 3], in1=held["x", u][:, :, 4], op=ALU.add)
-                held["last", u] = last_two[:]
+                held["rest", u] = last_two
+
+        def copy_x4(u):
+            if u >= THREE_TERM_UNITS:
+                x4 = work.tile([P, ROWS], BF16, tag="x4")
+                nc.scalar.copy(out=x4[:], in_=held["x", u][:, :, 4])
+                held["rest", u] = x4
 
         def compare(u):
             zero = work.tile([P, TILES, A], BF16, tag="zero", bufs=2)
             nc.vector.scalar_tensor_tensor(
-                out=zero[:].rearrange("p j a -> p (j a)"), in0=held.get(("last", u), held["x", u][:, :, 4]), scalar=-1.0,
-                in1=held["four", u][:], op0=ALU.mult, op1=ALU.is_equal,
+                out=zero[:].rearrange("p j a -> p (j a)"), in0=held["rest", u][:], scalar=-1.0, in1=held["four", u][:],
+                op0=ALU.mult, op1=ALU.is_equal,
             )
             held["zero", u] = zero
 
@@ -296,6 +302,7 @@ def tile_dqn_pa_t_kernel(tc, x, h1, W2, b2, W3, b3, out):
             run(first_product, k - 1, 2)
             run(quantise_h2, k - 2)
             run(add_b2, k - 1, 2)
+            run(copy_x4, k - 1)
             run(compare, k - 2)
             run(row_max, k - 3)
             run(second_product, k - 2)

from contextlib import ExitStack

import concourse.mybir as mybir
from concourse.masks import make_identity

F32 = mybir.dt.float32
BF16 = mybir.dt.bfloat16
U32 = mybir.dt.uint32
U8 = mybir.dt.uint8
FP8X4 = mybir.dt.float8_e4m3fn_x4
ALU = mybir.AluOpType
ACT = mybir.ActivationFunctionType
AX = mybir.AxisListType

P = 128
PACK = 4
B, A, G, H1, H2 = 8192, 128, 5, 1024, 512
SLOPE = 0.4
UNIT = 2.0**64
PASSES = H1 // (P * PACK)
TILES = 4
ROWS = P * TILES
UNITS = B // ROWS
AHEAD = 3
THREE_TERM_UNITS = 7
FLOPS = 2 * B * (H1 * H2 + H2 * A)


def tile_dqn_pa_t_kernel(tc, x, h1, W2, b2, W3, b3, out):
    nc = tc.nc
    with ExitStack() as ctx:
        const = ctx.enter_context(tc.tile_pool(name="const", bufs=1))
        loads = ctx.enter_context(tc.tile_pool(name="loads", bufs=AHEAD + 1))
        work = ctx.enter_context(tc.tile_pool(name="work", bufs=3))
        psum = ctx.enter_context(tc.psum_pool(name="psum", bufs=1))
        ctx.enter_context(tc.manual_schedule())
        held = {}

        def load_h1(u):
            rows = slice(ROWS * u, ROWS * (u + 1))
            h1_sb = loads.tile([P, TILES, H1], BF16, tag="h1")
            nc.sync.dma_start(out=h1_sb[:], in_=h1[rows, :].rearrange("(j p) k -> p j k", p=P))
            held["h1", u] = h1_sb

        def load_x(u):
            rows = slice(ROWS * u, ROWS * (u + 1))
            x_sb = loads.tile([P, TILES, A * G], BF16, tag="x", bufs=AHEAD + 2)
            nc.sync.dma_start(out=x_sb[:], in_=x[rows, :].rearrange("(p j) c -> p j c", j=TILES))
            held["x", u] = x_sb[:].rearrange("p j (a e) -> p (j a) e", e=G)

        load_h1(0)
        w2_raw = const.tile([P, PASSES, PACK * H2], BF16)
        nc.sync.dma_start(out=w2_raw[:], in_=W2.rearrange("(s q v) n -> q s (v n)", s=PASSES, v=PACK))
        b2_bf = const.tile([P, PACK], BF16)
        nc.sync.dma_start(out=b2_bf[:], in_=b2.rearrange("(p t) -> p t", t=PACK))
        load_h1(1)
        w3_raw = const.tile([P, PACK, A], BF16)
        nc.sync.dma_start(out=w3_raw[:], in_=W3.rearrange("(p t) a -> p t a", t=PACK))
        load_h1(2)
        load_x(0)
        b3_bf = const.tile([P, A], BF16)
        nc.sync.dma_start(out=b3_bf[:], in_=b3.partition_broadcast(P))

        ident_f32 = const.tile([P, P], F32)
        make_identity(nc, ident_f32[:])
        ident_bf = const.tile([P, P], BF16)
        make_identity(nc, ident_bf[:])

        w2_grouped = const.tile([P, PASSES, PACK * H2], BF16, align_bytes=64)
        w2_words = const.tile([P, PASSES, H2], U32, align_bytes=64)
        w2_scales = const.tile([P, PASSES, H2], U8, align_bytes=64)

        def group_w2(s, copy):
            copy(
                out=w2_grouped[:, s, :].rearrange("q (t m v) -> q t m v", t=PACK, v=PACK),
                in_=w2_raw[:, s, :].rearrange("q (v m t) -> q t m v", v=PACK, t=PACK),
            )

        def quantise_w2(s):
            nc.vector.quantize_mx(
                out=w2_words[:, s, :].bitcast(FP8X4), scales=w2_scales[:, s, :], in_=w2_grouped[:, s, :]
            )

        w3_grouped = const.tile([P, A, PACK], BF16, align_bytes=64)
        w3_words = const.tile([P, A], U32, align_bytes=64)
        w3_scales = const.tile([P, A], U8, align_bytes=64)
        b2_f32 = const.tile([P, PACK], F32)
        b3_units = const.tile([P, TILES, A], BF16)

        def prepare_w3_and_b3():
            nc.vector.tensor_copy(out=w3_grouped[:], in_=w3_raw[:].rearrange("p t a -> p a t"))
            nc.vector.tensor_scalar(
                out=b3_units[:], in0=b3_bf[:].unsqueeze(1).to_broadcast([P, TILES, A]), scalar1=1.0 / UNIT, scalar2=None,
                op0=ALU.mult,
            )
            nc.vector.quantize_mx(
                out=w3_words[:].bitcast(FP8X4), scales=w3_scales[:], in_=w3_grouped[:].rearrange("p a t -> p (a t)")
            )

        def transpose_h1(u, s, half):
            bank = psum.tile([P, 2, 2, P], F32, tag="bank", bufs=6)
            for j in range(2):
                for w in range(2):
                    nc.tensor.transpose(
                        bank[:, j, w, :],
                        held["h1", u][:, 2 * half + j, :].bitcast(F32)[:, 2 * P * s + w : 2 * P * (s + 1) : 2],
                        ident_f32[:],
                    )
            held["h1T", u, s, half] = bank

        def copy_h1T(u, s, half):
            if s == 0 and half == 0:
                grouped = work.tile([P, PASSES, PACK * ROWS], BF16, align_bytes=64, tag="grouped", bufs=2)
                held["grouped", u] = grouped
            words = held["grouped", u][:, s, :].bitcast(F32).rearrange("p (j r w) -> p j r w", j=TILES, w=2)
            nc.scalar.copy(
                out=words[:, 2 * half : 2 * half + 2],
                in_=held["h1T", u, s, half][:].rearrange("p j w r -> p j r w"),
            )

        def quantise_h1(u):
            h1_words = work.tile([P, PASSES, ROWS], U32, align_bytes=64, tag="h1_words")
            h1_scales = work.tile([P, PASSES, ROWS], U8, align_bytes=64, tag="h1_scales")
            nc.vector.quantize_mx(
                out=h1_words[:].rearrange("p s r -> p (s r)").bitcast(FP8X4),
                scales=h1_scales[:].rearrange("p s r -> p (s r)"),
                in_=held["grouped", u][:].rearrange("p s rt -> p (s rt)"),
            )
            held["h1_words", u] = h1_words
            held["h1_scales", u] = h1_scales

        def first_product(u, first_t):
            products = held.setdefault(("products", u), [])
            for t in range(first_t, first_t + 2):
                bank = psum.tile([P, ROWS], F32, tag="bank", bufs=6)
                for s in range(PASSES):
                    nc.tensor.matmul_mx(
                        out=bank[:],
                        lhsT=w2_words[:, s, P * t : P * (t + 1)].bitcast(FP8X4),
                        lhsT_scale=w2_scales[:, s, P * t : P * (t + 1)],
                        rhs=held["h1_words", u][:, s, :].bitcast(FP8X4),
                        rhs_scale=held["h1_scales", u][:, s, :],
                        start=(s == 0),
                        stop=(s == PASSES - 1),
                    )
                products.append(bank)

        def add_b2(u, first_t):
            if first_t == 0:
                v_new = work.tile([P, ROWS // 4, PACK, 4], F32, tag="v")
                held["v", u] = v_new
            v = held["v", u]
            for t in range(first_t, first_t + 2):
                nc.scalar.activation(
                    out=v[:, :, t, :],
                    in_=held["products", u][t][:].rearrange("p (c i) -> p c i", i=4),
                    func=ACT.Identity,
                    bias=b2_f32[:, t : t + 1],
                    scale=1.0,
                )

        def leaky(u):
            h2 = work.tile([P, TILES, PACK * P], BF16, align_bytes=64, tag="h2", bufs=3)
            v = held["v", u][:].rearrange("p c t i -> p (c t) i")
            nc.vector.scalar_tensor_tensor(
                out=h2[:].rearrange("p i ct -> p ct i"), in0=v, scalar=SLOPE, in1=v, op0=ALU.mult, op1=ALU.max
            )
            held["h2", u] = h2

        def quantise_h2(u):
            h2_words = work.tile([P, ROWS], U32, align_bytes=64, tag="h2_words")
            h2_scales = work.tile([P, ROWS], U8, align_bytes=64, tag="h2_scales")
            nc.vector.quantize_mx(
                out=h2_words[:].bitcast(FP8X4), scales=h2_scales[:], in_=held["h2", u][:].rearrange("p i ct -> p (i ct)")
            )
            held["h2_words", u] = h2_words
            held["h2_scales", u] = h2_scales

        def second_product(u):
            logits = psum.tile([P, TILES, A], F32, tag="logits")
            for j in range(TILES):
                nc.tensor.matmul_mx(
                    out=logits[:, j, :],
                    lhsT=held["h2_words", u][:, P * j : P * (j + 1)].bitcast(FP8X4),
                    lhsT_scale=held["h2_scales", u][:, P * j : P * (j + 1)],
                    rhs=w3_words[:].bitcast(FP8X4),
                    rhs_scale=w3_scales[:],
                    start=True,
                    stop=True,
                )
            held["logits", u] = logits

        def sum_on_tensor(u, e):
            terms = 3 if u < THREE_TERM_UNITS else 4
            if e == 0:
                part = psum.tile([P, ROWS], F32, tag="part")
                held["four", u] = part
            if e < terms:
                nc.tensor.matmul(
                    out=held["four", u][:], lhsT=ident_bf[:], rhs=held["x", u][:, :, e], start=(e == 0),
                    stop=(e == terms - 1),
                )

        def sum_last_two(u):
            if u < THREE_TERM_UNITS:
                last_two = work.tile([P, ROWS], F32, align_bytes=64, tag="h2", bufs=3)
                nc.gpsimd.tensor_tensor(out=last_two[:], in0=held["x", u][:, :, 3], in1=held["x", u][:, :, 4], op=ALU.add)
                held["rest", u] = last_two

        def copy_x4(u):
            if u >= THREE_TERM_UNITS:
                x4 = work.tile([P, ROWS], BF16, tag="x4")
                nc.scalar.copy(out=x4[:], in_=held["x", u][:, :, 4])
                held["rest", u] = x4

        def compare(u):
            zero = work.tile([P, TILES, A], BF16, tag="zero", bufs=2)
            nc.vector.scalar_tensor_tensor(
                out=zero[:].rearrange("p j a -> p (j a)"), in0=held["rest", u][:], scalar=-1.0, in1=held["four", u][:],
                op0=ALU.mult, op1=ALU.is_equal,
            )
            held["zero", u] = zero

        def offsets(u):
            offset = work.tile([P, TILES, A], BF16, tag="offset", bufs=5)
            nc.vector.tensor_tensor(out=offset[:], in0=b3_units[:], in1=held["zero", u][:], op=ALU.subtract)
            held["offset", u] = offset

        def masked_logits(u):
            masked = work.tile([P, TILES, A], F32, tag="masked")
            nc.vector.scalar_tensor_tensor(
                out=masked[:], in0=held["logits", u][:], scalar=1.0 / UNIT, in1=held["offset", u][:], op0=ALU.mult, op1=ALU.add
            )
            held["masked", u] = masked

        def row_max(u):
            minus_max = work.tile([P, TILES], F32, tag="minus_max")
            nc.vector.tensor_reduce(out=minus_max[:], in_=held["masked", u][:], axis=AX.X, op=ALU.max, negate=True)
            held["minus_max", u] = minus_max

        def scale_max(u):
            bias = work.tile([P, TILES], F32, tag="bias")
            nc.scalar.activation(out=bias[:], in_=held["minus_max", u][:], func=ACT.Copy, scale=UNIT)
            held["bias", u] = bias

        def exponentials(u):
            expo = work.tile([P, TILES, A], F32, tag="expo")
            total = work.tile([P, TILES], F32, tag="total")
            for j in range(TILES):
                nc.scalar.activation(
                    out=expo[:, j, :], in_=held["masked", u][:, j, :], func=ACT.Exp,
                    bias=held["bias", u][:, j : j + 1], scale=UNIT, accum_out=total[:, j : j + 1],
                )
            held["expo", u] = expo
            held["total", u] = total

        def reciprocals(u):
            inverse = work.tile([P, TILES], F32, tag="inverse")
            nc.vector.reciprocal(out=inverse[:], in_=held["total", u][:])
            held["inverse", u] = inverse

        def scale_and_store(u):
            probs = work.tile([P, TILES, A], F32, tag="probs")
            for j in range(TILES):
                nc.scalar.activation(
                    out=probs[:, j, :], in_=held["expo", u][:, j, :], func=ACT.Copy,
                    scale=held["inverse", u][:, j : j + 1],
                )
            rows = slice(ROWS * u, ROWS * (u + 1))
            nc.sync.dma_start(out=out[rows, :].rearrange("(p j) a -> p j a", j=TILES), in_=probs[:])

        def run(stage, u, *part):
            if 0 <= u < UNITS:
                stage(u, *part)

        group_w2(0, nc.vector.tensor_copy)
        nc.vector.tensor_copy(out=b2_f32[:], in_=b2_bf[:])
        quantise_w2(0)
        for k in range(UNITS + 5):
            run(load_h1, k + AHEAD)
            run(load_x, k + 1)
            run(sum_last_two, k - 2)
            run(leaky, k - 2)
            run(scale_max, k - 4)
            run(transpose_h1, k, 0, 0)
            run(copy_h1T, k, 0, 0)
            run(sum_on_tensor, k - 2, 0)
            run(transpose_h1, k, 0, 1)
            run(copy_h1T, k, 0, 1)
            run(exponentials, k - 4)
            run(sum_on_tensor, k - 2, 1)
            run(transpose_h1, k, 1, 0)
            run(copy_h1T, k, 1, 0)
            run(sum_on_tensor, k - 2, 2)
            run(transpose_h1, k, 1, 1)
            run(copy_h1T, k, 1, 1)
            run(scale_and_store, k - 5)
            run(sum_on_tensor, k - 2, 3)
            run(masked_logits, k - 3)
            run(first_product, k - 1, 0)
            run(add_b2, k - 1, 0)
            run(first_product, k - 1, 2)
            run(quantise_h2, k - 2)
            run(add_b2, k - 1, 2)
            run(copy_x4, k - 1)
            run(compare, k - 2)
            run(row_max, k - 3)
            run(second_product, k - 2)
            run(quantise_h1, k)
            if k == 0:
                group_w2(1, nc.scalar.copy)
                quantise_w2(1)
            if k == 1:
                prepare_w3_and_b3()
            run(offsets, k - 2)
            run(reciprocals, k - 4)
